import numpy as np
import ml_dtypes


def mxq(x, axis, fmt="e4m3"):
    dtype, down = {"e4m3": (ml_dtypes.float8_e4m3fn, 7), "e5m2": (ml_dtypes.float8_e5m2, 14)}[fmt]
    v = np.moveaxis(np.asarray(x, np.float32).astype(ml_dtypes.bfloat16).astype(np.float64), axis, -1)
    blocks = v.reshape(v.shape[:-1] + (-1, 32))
    amax = np.abs(blocks).max(-1, keepdims=True)
    byte = np.maximum(np.where(amax > 0, np.frexp(amax)[1] - 1 + 127, 0) - down, 1)
    scale = np.exp2(byte - 127.0)
    codes = (blocks / scale).astype(np.float32).astype(dtype).astype(np.float64)
    return np.moveaxis((codes * scale).reshape(v.shape), -1, axis)


WIDE = False


def mx_kscale(k):
    if not WIDE:
        return np.ones(k)
    levels = np.array([10, -10, 5, -5, 0])
    a = np.random.permutation(np.resize(levels, k // 512 * 4)).reshape(k // 512, 4)
    idx = np.arange(k)
    return np.exp2(a[idx // 512, idx % 128 // 32])


BF16 = ml_dtypes.bfloat16


def bf(x):
    return np.asarray(x, np.float32).astype(BF16)


def f64(x):
    return np.asarray(x).astype(np.float64)


E2M1 = np.array([0.0, 0.5, 1.0, 1.5, 2.0, 3.0, 4.0, 6.0, -0.0, -0.5, -1.0, -1.5, -2.0, -3.0, -4.0, -6.0])


def pack_weight(w, fmt):
    k, n = w.shape
    w = f64(bf(w)).reshape(k // 32, 32, n)
    amax = np.abs(w).max(1)
    if fmt == "e4m3":
        byte = np.frexp(amax)[1] - 1 + 127 - 7
    else:
        mant, ex = np.frexp(amax / 6.0)
        byte = np.where(mant > 0.5, ex, ex - 1) + 127
    byte = np.clip(np.where(amax > 0, byte, 1), 1, 254)
    scaled = (w * np.exp2(127.0 - byte)[:, None, :]).reshape(k, n).astype(np.float32)
    by_word = np.ascontiguousarray(scaled.reshape(k // 512, 128, 4, n).transpose(0, 1, 3, 2))
    if fmt == "e4m3":
        words = by_word.astype(ml_dtypes.float8_e4m3fn).view(np.uint8)
    else:
        c = by_word.astype(ml_dtypes.float4_e2m1fn).view(np.uint8) & 0xF
        words = c[..., 0::2] | (c[..., 1::2] << 4)
    return np.ascontiguousarray(words), np.ascontiguousarray(byte.astype(np.uint8).reshape(k // 512, 16, n))


def unpack_weight(words, scales, fmt):
    g, p, n, _ = words.shape
    if fmt == "e4m3":
        vals = np.ascontiguousarray(words).view(ml_dtypes.float8_e4m3fn).astype(np.float64)
    else:
        nib = np.empty((g, p, n, 4), np.uint8)
        nib[..., 0::2] = words & 0xF
        nib[..., 1::2] = words >> 4
        vals = E2M1[nib]
    vals = vals * np.repeat(np.exp2(scales.astype(np.float64) - 127.0), 8, axis=1)[..., None]
    return vals.transpose(0, 1, 3, 2).reshape(g * 512, n)


B, S, HID, NH, NKV, DH = 2, 128, 16384, 8, 2, 128
EPS = 1e-6
WAVELENGTH = 10000.0
PRE = 4.5 * np.sqrt(EPS)
FMT = "e4m3"


def rms_norm(x, scale=None):
    out = x * (1.0 / np.sqrt(np.mean(x * x, axis=-1, keepdims=True) + EPS))
    if scale is not None:
        out = out * scale
    return out


def rope(x):
    inv_freq = 1.0 / WAVELENGTH ** (np.arange(0, DH, 2) / DH)
    freq = np.arange(S)[:, None] * inv_freq[None, :]
    emb = np.concatenate([freq, freq], axis=-1)
    cos = np.cos(emb)[None, :, None, :]
    sin = np.sin(emb)[None, :, None, :]
    x1, x2 = np.split(x, 2, axis=-1)
    rot = np.concatenate([-x2, x1], axis=-1)
    return x * cos + rot * sin


def setup_inputs():
    s = mx_kscale(HID)
    c = PRE / np.sqrt(HID)
    hidden_states = bf(np.random.standard_normal((B, S, HID)) * s)
    wq_words, wq_scales = pack_weight(np.random.standard_normal((HID, NH * DH)) * c / s[:, None], FMT)
    wk_words, wk_scales = pack_weight(np.random.standard_normal((HID, NKV * DH)) * c / s[:, None], FMT)
    wv_words, wv_scales = pack_weight(np.random.standard_normal((HID, NKV * DH)) * c / s[:, None], FMT)
    q_scale = bf(1.0 + 0.1 * np.random.standard_normal(DH))
    k_scale = bf(1.0 + 0.1 * np.random.standard_normal(DH))
    return {"hidden_states": hidden_states,
            "wq_words": wq_words, "wq_scales": wq_scales,
            "wk_words": wk_words, "wk_scales": wk_scales,
            "wv_words": wv_words, "wv_scales": wv_scales,
            "q_scale": q_scale,
            "k_scale": k_scale}


def reference(hidden_states, wq_words, wq_scales, wk_words, wk_scales, wv_words, wv_scales, q_scale, k_scale):
    xq = mxq(f64(hidden_states), 2, "e4m3")
    q = (xq @ unpack_weight(wq_words, wq_scales, FMT)).reshape(B, S, NH, DH)
    k = (xq @ unpack_weight(wk_words, wk_scales, FMT)).reshape(B, S, NKV, DH)
    v = (xq @ unpack_weight(wv_words, wv_scales, FMT)).reshape(B, S, NKV, DH)
    q = rope(rms_norm(q, f64(q_scale)))
    k = rope(rms_norm(k, f64(k_scale)))
    v = rms_norm(v)
    return q, k, v

@@ -1,0 +1,332 @@
+import math
+from contextlib import ExitStack
+
+import concourse.mybir as mybir
+from concourse.masks import make_identity
+
+F32 = mybir.dt.float32
+BF16 = mybir.dt.bfloat16
+I32 = mybir.dt.int32
+U8 = mybir.dt.uint8
+FP8X4 = mybir.dt.float8_e4m3fn_x4
+ALU = mybir.AluOpType
+ACT = mybir.ActivationFunctionType
+
+P = 128
+BATCH = 2
+HIDDEN = 16384
+HEAD = 128
+HALF = HEAD // 2
+Q_HEADS = 8
+KV_HEADS = 2
+EPS = 1e-6
+WAVELENGTH = 10000.0
+
+K_PASS = 512
+GROUPS = HIDDEN // K_PASS
+BANK = 512
+
+X_GROUPS = 8
+BANK_GROUPS = 2
+X_BANKS = X_GROUPS // BANK_GROUPS
+WQ_GROUPS = 2
+WKV_GROUPS = 4
+
+PLANES = 4
+SLOTS = GROUPS // PLANES
+
+FLOPS = 2 * BATCH * P * HIDDEN * (Q_HEADS + 2 * KV_HEADS) * HEAD
+
+TWO_PI_HIGH = 6.28125
+TWO_PI_MID = 0.0019350051879882812
+TWO_PI_LOW = 2.0 * math.pi - TWO_PI_HIGH - TWO_PI_MID
+ROUND_TO_WHOLE = 12582912.0
+
+
+def load_scale_planes(nc, planes, scales):
+    for plane in range(PLANES):
+        groups = slice(plane * SLOTS, (plane + 1) * SLOTS)
+        for quadrant in range(4):
+            first = 32 * quadrant + 4 * plane
+            nc.gpsimd.dma_start(
+                out=planes[first : first + 4, :, :].bitcast(F32),
+                in_=scales[groups, 4 * quadrant : 4 * quadrant + 4, :]
+                .rearrange("j r n -> r j n")
+                .bitcast(F32),
+            )
+
+
+def plane_of(planes, group, columns):
+    return planes[4 * (group // SLOTS) : P, group % SLOTS, columns]
+
+
+def tile_gemma3ntextattention_pa_k_kernel(
+    tc,
+    hidden_states,
+    wq_words,
+    wq_scales,
+    wk_words,
+    wk_scales,
+    wv_words,
+    wv_scales,
+    q_scale,
+    k_scale,
+    out_0,
+    out_1,
+    out_2,
+):
+    nc = tc.nc
+    with ExitStack() as ctx:
+        ctx.enter_context(tc.manual_schedule())
+        keep = ctx.enter_context(tc.tile_pool(name="keep", bufs=1))
+        x_pool = ctx.enter_context(tc.tile_pool(name="x_pool", bufs=6))
+        grouped_pool = ctx.enter_context(tc.tile_pool(name="grouped_pool", bufs=2))
+        wq_pool = ctx.enter_context(tc.tile_pool(name="wq_pool", bufs=5))
+        wkv_pool = ctx.enter_context(tc.tile_pool(name="wkv_pool", bufs=8))
+        work = ctx.enter_context(tc.tile_pool(name="work", bufs=2))
+
+        gain_rows = keep.tile([P, 2 * HEAD], BF16)
+        nc.vector.memset(gain_rows[:], 0.0)
+        ones = keep.tile([P, P], BF16)
+        nc.vector.memset(ones[:], 1.0)
+        nc.scalar.dma_start(out=gain_rows[0:1, 0:HEAD], in_=q_scale.unsqueeze(0))
+        nc.scalar.dma_start(out=gain_rows[0:1, HEAD : 2 * HEAD], in_=k_scale.unsqueeze(0))
+
+        identity = keep.tile([P, P], F32)
+        make_identity(nc, identity[:])
+        position_int = keep.tile([P, 1], I32)
+        nc.gpsimd.iota(position_int[:], pattern=[[0, 1]], base=0, channel_multiplier=1)
+
+        wq_planes = keep.tile([P, SLOTS, Q_HEADS * HEAD], U8, align_bytes=64)
+        wk_planes = keep.tile([P, SLOTS, KV_HEADS * HEAD], U8, align_bytes=64)
+        wv_planes = keep.tile([P, SLOTS, KV_HEADS * HEAD], U8, align_bytes=64)
+        for planes, scales in ((wq_planes, wq_scales), (wk_planes, wk_scales), (wv_planes, wv_scales)):
+            nc.vector.memset(planes[:].rearrange("p j n -> p (j n)").bitcast(I32), 0)
+            load_scale_planes(nc, planes, scales)
+
+        x_codes = keep.tile([P, BATCH, GROUPS, P], I32, align_bytes=64)
+        x_planes = keep.tile([P, BATCH, GROUPS, P], U8, align_bytes=64)
+
+        def quantise(grouped, b, first_group):
+            groups = slice(first_group, first_group + X_GROUPS)
+            nc.vector.quantize_mx(
+                out=x_codes[:, b, groups, :].rearrange("p g m -> p (g m)").bitcast(FP8X4),
+                scales=x_planes[:, b, groups, :].rearrange("p g m -> p (g m)"),
+                in_=grouped[:].rearrange("p g m t -> p (g m t)"),
+            )
+
+        with tc.psum_pool(name="transposed", bufs=2 * X_BANKS, reuse_waits="tile") as transposed:
+            waiting = None
+            for b in range(BATCH):
+                for first_group in range(0, GROUPS, X_GROUPS):
+                    x_rows = x_pool.tile([P, X_GROUPS * K_PASS], BF16)
+                    nc.sync.dma_start(
+                        out=x_rows[:],
+                        in_=hidden_states[
+                            b, :, first_group * K_PASS : (first_group + X_GROUPS) * K_PASS
+                        ],
+                    )
+                    x_words = x_rows[:].bitcast(F32)
+                    banks = []
+                    for i in range(X_BANKS):
+                        bank = transposed.tile([P, BANK_GROUPS, 2, P], F32, name="bank")
+                        banks.append(bank)
+                        for j in range(BANK_GROUPS):
+                            start = (i * BANK_GROUPS + j) * (K_PASS // 2)
+                            for u in range(2):
+                                nc.tensor.transpose(
+                                    bank[:, j, u, :],
+                                    x_words[:, start + u : start + K_PASS // 2 : 2],
+                                    identity[:],
+                                )
+                    if waiting is not None:
+                        quantise(*waiting)
+                    grouped = grouped_pool.tile([P, X_GROUPS, P, 4], BF16, align_bytes=64)
+                    for i in range(X_BANKS):
+                        target = (
+                            grouped[:, i * BANK_GROUPS : (i + 1) * BANK_GROUPS, :, :]
+                            .rearrange("p g m t -> p g (m t)")
+                            .bitcast(F32)
+                            .rearrange("p g (m u) -> p g m u", u=2)
+                        )
+                        source = banks[i][:].rearrange("p g u m -> p g m u")
+                        if i == X_BANKS - 1:
+                            nc.vector.tensor_copy(out=target, in_=source)
+                        else:
+                            nc.scalar.copy(out=target, in_=source)
+                    waiting = (grouped, b, first_group)
+            quantise(*waiting)
+
+        with tc.psum_pool(name="sums_psum", bufs=1, reuse_waits="tile") as sums_psum:
+            q_acc = [
+                [sums_psum.tile([P, BANK], F32, name="q_acc_%d_%d" % (b, c)) for c in range(2)]
+                for b in range(BATCH)
+            ]
+            v_acc = [sums_psum.tile([P, BANK], F32, name="v_acc_%d" % b) for b in range(BATCH)]
+            k_acc = [sums_psum.tile([P, BANK], F32, name="k_acc_%d" % b) for b in range(BATCH)]
+
+            gains = keep.tile([P, 2, 2, HALF], F32)
+            spare = v_acc[0][:, BANK - 2 * HEAD : BANK]
+            nc.tensor.matmul(out=spare, lhsT=ones[:], rhs=gain_rows[:], start=True, stop=True)
+            nc.vector.tensor_copy(out=gains[:].rearrange("p w h d -> p (w h d)"), in_=spare)
+
+            inv_freq = keep.tile([P, HALF], F32)
+            nc.vector.memset(inv_freq[:, 0:1], 1.0)
+            width = 1
+            while width < HALF:
+                nc.vector.tensor_scalar_mul(
+                    out=inv_freq[:, width : 2 * width],
+                    in0=inv_freq[:, 0:width],
+                    scalar1=WAVELENGTH ** (-width / HALF),
+                )
+                width *= 2
+            position = keep.tile([P, 1], F32)
+            nc.vector.tensor_copy(out=position[:], in_=position_int[:])
+            angle = keep.tile([P, HALF], F32)
+            nc.vector.tensor_scalar_mul(out=angle[:], in0=inv_freq[:], scalar1=position[:, 0:1])
+            turns = keep.tile([P, HALF], F32)
+            nc.vector.tensor_scalar(
+                out=turns[:],
+                in0=angle[:],
+                scalar1=1.0 / (2.0 * math.pi),
+                scalar2=ROUND_TO_WHOLE,
+                op0=ALU.mult,
+                op1=ALU.add,
+            )
+            nc.vector.tensor_scalar_add(out=turns[:], in0=turns[:], scalar1=-ROUND_TO_WHOLE)
+            for piece in (TWO_PI_HIGH, TWO_PI_MID, TWO_PI_LOW):
+                nc.vector.scalar_tensor_tensor(
+                    out=angle[:], in0=turns[:], scalar=-piece, in1=angle[:], op0=ALU.mult, op1=ALU.add
+                )
+            angle_abs = keep.tile([P, HALF], F32)
+            nc.vector.scalar_tensor_tensor(
+                out=angle_abs[:], in0=angle[:], scalar=-1.0, in1=angle[:], op0=ALU.mult, op1=ALU.max
+            )
+            sin = keep.tile([P, HALF], F32)
+            nc.scalar.activation(out=sin[:], in_=angle[:], func=ACT.Sin)
+            cos = keep.tile([P, HALF], F32)
+            nc.scalar.activation(out=cos[:], in_=angle_abs[:], func=ACT.Sin, bias=math.pi / 2.0, scale=-1.0)
+            same = keep.tile([P, 2, 2, HALF], F32)
+            other = keep.tile([P, 2, 2, HALF], F32)
+            for w in range(2):
+                nc.vector.tensor_tensor(
+                    out=same[:, w, :, :],
+                    in0=gains[:, w, :, :],
+                    in1=cos[:].unsqueeze(1).to_broadcast([P, 2, HALF]),
+                    op=ALU.mult,
+                )
+                nc.vector.scalar_tensor_tensor(
+                    out=other[:, w, 0, :], in0=gains[:, w, 1, :], scalar=-1.0, in1=sin[:], op0=ALU.mult, op1=ALU.mult
+                )
+                nc.vector.tensor_tensor(out=other[:, w, 1, :], in0=gains[:, w, 0, :], in1=sin[:], op=ALU.mult)
+
+            def normalised(acc, heads):
+                squares = work.tile([P, BANK], F32, name="squares")
+                sums = work.tile([P, 4], F32, name="sums")
+                for h in range(heads):
+                    columns = slice(h * HEAD, (h + 1) * HEAD)
+                    nc.scalar.activation(
+                        out=squares[:, columns], in_=acc[:, columns], func=ACT.Square, accum_out=sums[:, h : h + 1]
+                    )
+                rms = work.tile([P, 4], F32, name="rms")
+                nc.scalar.activation(
+                    out=rms[:, 0:heads], in_=sums[:, 0:heads], func=ACT.Sqrt, bias=EPS, scale=1.0 / HEAD
+                )
+                inverse = work.tile([P, 4], F32, name="inverse")
+                nc.vector.reciprocal(out=inverse[:, 0:heads], in_=rms[:, 0:heads])
+                unit = work.tile([P, 4, HEAD], F32, name="unit")
+                nc.vector.tensor_tensor(
+                    out=unit[:, 0:heads, :],
+                    in0=acc[:, 0 : heads * HEAD].rearrange("p (h d) -> p h d", d=HEAD),
+                    in1=inverse[:, 0:heads].unsqueeze(2).to_broadcast([P, heads, HEAD]),
+                    op=ALU.mult,
+                )
+                return unit
+
+            def rotated(unit, heads, w):
+                halves = unit[:, 0:heads, :].rearrange("p h (s d) -> p h s d", s=2)
+                turned = work.tile([P, 4, 2, HALF], F32, name="turned")
+                crossed = work.tile([P, 4, 2, HALF], F32, name="crossed")
+                nc.vector.tensor_tensor(
+                    out=turned[:, 0:heads, :, :].rearrange("p h s d -> p h (s d)"),
+                    in0=unit[:, 0:heads, :],
+                    in1=same[:, w, :, :].rearrange("p s d -> p (s d)").unsqueeze(1).to_broadcast([P, heads, HEAD]),
+                    op=ALU.mult,
+                )
+                for s in range(2):
+                    nc.vector.tensor_tensor(
+                        out=crossed[:, 0:heads, s, :],
+                        in0=halves[:, :, 1 - s, :],
+                        in1=other[:, w, s, :].unsqueeze(1).to_broadcast([P, heads, HALF]),
+                        op=ALU.mult,
+                    )
+                nc.vector.tensor_tensor(
+                    out=turned[:, 0:heads, :, :], in0=turned[:, 0:heads, :, :], in1=crossed[:, 0:heads, :, :], op=ALU.add
+                )
+                return turned
+
+            for first_group in range(0, GROUPS, WQ_GROUPS):
+                words = wq_pool.tile([P, WQ_GROUPS, Q_HEADS * HEAD], I32, name="wq_tile", align_bytes=64)
+                nc.sync.dma_start(
+                    out=words[:],
+                    in_=wq_words[first_group : first_group + WQ_GROUPS]
+                    .rearrange("g p n t -> p g (n t)")
+                    .bitcast(I32),
+                )
+                for j in range(WQ_GROUPS):
+                    g = first_group + j
+                    for b in range(BATCH):
+                        for c in range(2):
+                            columns = slice(c * BANK, (c + 1) * BANK)
+                            nc.tensor.matmul_mx(
+                                out=q_acc[b][c][:],
+                                lhsT=x_codes[:, b, g, :].bitcast(FP8X4),
+                                lhsT_scale=x_planes[:, b, g, :],
+                                rhs=words[:, j, columns].bitcast(FP8X4),
+                                rhs_scale=plane_of(wq_planes, g, columns),
+                                start=(g == 0),
+                                stop=(g == GROUPS - 1),
+                            )
+            for b in range(BATCH):
+                for c in range(2):
+                    result = rotated(normalised(q_acc[b][c], 4), 4, 0)
+                    nc.gpsimd.dma_start(
+                        out=out_0[b, :, 4 * c : 4 * c + 4, :].rearrange("s h d -> s (h d)"),
+                        in_=result[:].rearrange("p h s d -> p (h s d)"),
+                    )
+
+            kv_width = KV_HEADS * HEAD
+            for w_words, planes, acc in ((wk_words, wk_planes, k_acc), (wv_words, wv_planes, v_acc)):
+                for first_group in range(0, GROUPS, WKV_GROUPS):
+                    words = wkv_pool.tile([P, WKV_GROUPS, kv_width], I32, name="wkv_tile", align_bytes=64)
+                    nc.sync.dma_start(
+                        out=words[:],
+                        in_=w_words[first_group : first_group + WKV_GROUPS]
+                        .rearrange("g p n t -> p g (n t)")
+                        .bitcast(I32),
+                    )
+                    for b in range(BATCH):
+                        for j in range(WKV_GROUPS):
+                            g = first_group + j
+                            nc.tensor.matmul_mx(
+                                out=acc[b][:, 0:kv_width],
+                                lhsT=x_codes[:, b, g, :].bitcast(FP8X4),
+                                lhsT_scale=x_planes[:, b, g, :],
+                                rhs=words[:, j, :].bitcast(FP8X4),
+                                rhs_scale=plane_of(planes, g, slice(0, kv_width)),
+                                start=(g == 0),
+                                stop=(g == GROUPS - 1),
+                            )
+                if acc is k_acc:
+                    for b in range(BATCH):
+                        result = rotated(normalised(k_acc[b], KV_HEADS), KV_HEADS, 1)
+                        nc.gpsimd.dma_start(
+                            out=out_1[b].rearrange("s h d -> s (h d)"),
+                            in_=result[:, 0:KV_HEADS, :, :].rearrange("p h s d -> p (h s d)"),
+                        )
+            for b in range(BATCH):
+                result = normalised(v_acc[b], KV_HEADS)
+                nc.sync.dma_start(
+                    out=out_2[b].rearrange("s h d -> s (h d)"),
+                    in_=result[:, 0:KV_HEADS, :].rearrange("p h d -> p (h d)"),
+                )

@@ -43,21 +43,17 @@ TWO_PI_LOW = 2.0 * math.pi - TWO_PI_HIGH - TWO_PI_MID
 ROUND_TO_WHOLE = 12582912.0
 
 
-def load_scale_planes(nc, planes, scales):
-    for plane in range(PLANES):
-        groups = slice(plane * SLOTS, (plane + 1) * SLOTS)
-        for quadrant in range(4):
-            first = 32 * quadrant + 4 * plane
-            nc.gpsimd.dma_start(
-                out=planes[first : first + 4, :, :].bitcast(F32),
-                in_=scales[groups, 4 * quadrant : 4 * quadrant + 4, :]
-                .rearrange("j r n -> r j n")
-                .bitcast(F32),
-            )
+def load_plane_slot(nc, planes, scales, slot):
+    groups = slice(PLANES * slot, PLANES * (slot + 1))
+    for quadrant in range(4):
+        nc.sync.dma_start(
+            out=planes[32 * quadrant : 32 * quadrant + 4 * PLANES, slot, :].bitcast(I32),
+            in_=scales[groups, 4 * quadrant : 4 * quadrant + 4, :].bitcast(I32),
+        )
 
 
 def plane_of(planes, group, columns):
-    return planes[4 * (group // SLOTS) : P, group % SLOTS, columns]
+    return planes[4 * (group % PLANES) : P, group // PLANES, columns]
 
 
 def tile_gemma3ntextattention_pa_k_kernel(
@@ -85,6 +81,12 @@ def tile_gemma3ntextattention_pa_k_kernel(
         wkv_pool = ctx.enter_context(tc.tile_pool(name="wkv_pool", bufs=8))
         work = ctx.enter_context(tc.tile_pool(name="work", bufs=2))
 
+        wq_planes = keep.tile([P, SLOTS, Q_HEADS * HEAD], U8, align_bytes=64)
+        wk_planes = keep.tile([P, SLOTS, KV_HEADS * HEAD], U8, align_bytes=64)
+        wv_planes = keep.tile([P, SLOTS, KV_HEADS * HEAD], U8, align_bytes=64)
+        for planes in (wq_planes, wk_planes, wv_planes):
+            nc.vector.memset(planes[:].rearrange("p j n -> p (j n)").bitcast(I32), 0)
+
         gain_rows = keep.tile([P, 2 * HEAD], BF16)
         nc.vector.memset(gain_rows[:], 0.0)
         ones = keep.tile([P, P], BF16)
@@ -97,12 +99,6 @@ def tile_gemma3ntextattention_pa_k_kernel(
         position_int = keep.tile([P, 1], I32)
         nc.gpsimd.iota(position_int[:], pattern=[[0, 1]], base=0, channel_multiplier=1)
 
-        wq_planes = keep.tile([P, SLOTS, Q_HEADS * HEAD], U8, align_bytes=64)
-        wk_planes = keep.tile([P, SLOTS, KV_HEADS * HEAD], U8, align_bytes=64)
-        wv_planes = keep.tile([P, SLOTS, KV_HEADS * HEAD], U8, align_bytes=64)
-        for planes, scales in ((wq_planes, wq_scales), (wk_planes, wk_scales), (wv_planes, wv_scales)):
-            nc.vector.memset(planes[:].rearrange("p j n -> p (j n)").bitcast(I32), 0)
-            load_scale_planes(nc, planes, scales)
 
         x_codes = keep.tile([P, BATCH, GROUPS, P], I32, align_bytes=64)
         x_planes = keep.tile([P, BATCH, GROUPS, P], U8, align_bytes=64)
@@ -126,6 +122,7 @@ def tile_gemma3ntextattention_pa_k_kernel(
                             b, :, first_group * K_PASS : (first_group + X_GROUPS) * K_PASS
                         ],
                     )
+                    load_plane_slot(nc, wq_planes, wq_scales, (b * GROUPS + first_group) // X_GROUPS)
                     x_words = x_rows[:].bitcast(F32)
                     banks = []
                     for i in range(X_BANKS):
@@ -273,6 +270,11 @@ def tile_gemma3ntextattention_pa_k_kernel(
                     .rearrange("g p n t -> p g (n t)")
                     .bitcast(I32),
                 )
+                load_number = first_group // WQ_GROUPS
+                if load_number < SLOTS:
+                    load_plane_slot(nc, wk_planes, wk_scales, load_number)
+                else:
+                    load_plane_slot(nc, wv_planes, wv_scales, load_number - SLOTS)
                 for j in range(WQ_GROUPS):
                     g = first_group + j
                     for b in range(BATCH):

@@ -43,12 +43,13 @@ TWO_PI_LOW = 2.0 * math.pi - TWO_PI_HIGH - TWO_PI_MID
 ROUND_TO_WHOLE = 12582912.0
 
 
-def load_plane_slot(nc, planes, scales, slot):
-    groups = slice(PLANES * slot, PLANES * (slot + 1))
-    for quadrant in range(4):
+def load_scale_rows(nc, planes, scales, rows):
+    by_row = scales.rearrange("(j k) q n -> q k j n", k=PLANES)
+    for row in rows:
+        first = 32 * (row // 4) + row % 4
         nc.sync.dma_start(
-            out=planes[32 * quadrant : 32 * quadrant + 4 * PLANES, slot, :].bitcast(I32),
-            in_=scales[groups, 4 * quadrant : 4 * quadrant + 4, :].bitcast(I32),
+            out=planes[first : first + 4 * PLANES : 4, :, :].bitcast(I32),
+            in_=by_row[row].bitcast(I32),
         )
 
 
@@ -122,7 +123,8 @@ def tile_gemma3ntextattention_pa_k_kernel(
                             b, :, first_group * K_PASS : (first_group + X_GROUPS) * K_PASS
                         ],
                     )
-                    load_plane_slot(nc, wq_planes, wq_scales, (b * GROUPS + first_group) // X_GROUPS)
+                    load_number = (b * GROUPS + first_group) // X_GROUPS
+                    load_scale_rows(nc, wq_planes, wq_scales, (2 * load_number, 2 * load_number + 1))
                     x_words = x_rows[:].bitcast(F32)
                     banks = []
                     for i in range(X_BANKS):
@@ -271,10 +273,11 @@ def tile_gemma3ntextattention_pa_k_kernel(
                     .bitcast(I32),
                 )
                 load_number = first_group // WQ_GROUPS
-                if load_number < SLOTS:
-                    load_plane_slot(nc, wk_planes, wk_scales, load_number)
+                rows = (2 * load_number % 16, 2 * load_number % 16 + 1)
+                if load_number < 8:
+                    load_scale_rows(nc, wk_planes, wk_scales, rows)
                 else:
-                    load_plane_slot(nc, wv_planes, wv_scales, load_number - SLOTS)
+                    load_scale_rows(nc, wv_planes, wv_scales, rows)
                 for j in range(WQ_GROUPS):
                     g = first_group + j
                     for b in range(BATCH):

@@ -123,8 +123,11 @@ def tile_gemma3ntextattention_pa_k_kernel(
                             b, :, first_group * K_PASS : (first_group + X_GROUPS) * K_PASS
                         ],
                     )
-                    load_number = (b * GROUPS + first_group) // X_GROUPS
-                    load_scale_rows(nc, wq_planes, wq_scales, (2 * load_number, 2 * load_number + 1))
+                    if b == 0 and first_group == 0:
+                        for row in range(16):
+                            load_scale_rows(nc, wq_planes, wq_scales, (row,))
+                            load_scale_rows(nc, wk_planes, wk_scales, (row,))
+                            load_scale_rows(nc, wv_planes, wv_scales, (row,))
                     x_words = x_rows[:].bitcast(F32)
                     banks = []
                     for i in range(X_BANKS):
@@ -272,12 +275,6 @@ def tile_gemma3ntextattention_pa_k_kernel(
                     .rearrange("g p n t -> p g (n t)")
                     .bitcast(I32),
                 )
-                load_number = first_group // WQ_GROUPS
-                rows = (2 * load_number % 16, 2 * load_number % 16 + 1)
-                if load_number < 8:
-                    load_scale_rows(nc, wk_planes, wk_scales, rows)
-                else:
-                    load_scale_rows(nc, wv_planes, wv_scales, rows)
                 for j in range(WQ_GROUPS):
                     g = first_group + j
                     for b in range(BATCH):

@@ -76,7 +76,7 @@ def tile_gemma3ntextattention_pa_k_kernel(
     with ExitStack() as ctx:
         ctx.enter_context(tc.manual_schedule())
         keep = ctx.enter_context(tc.tile_pool(name="keep", bufs=1))
-        x_pool = ctx.enter_context(tc.tile_pool(name="x_pool", bufs=6))
+        x_pool = ctx.enter_context(tc.tile_pool(name="x_pool", bufs=4))
         grouped_pool = ctx.enter_context(tc.tile_pool(name="grouped_pool", bufs=2))
         wq_pool = ctx.enter_context(tc.tile_pool(name="wq_pool", bufs=5))
         wkv_pool = ctx.enter_context(tc.tile_pool(name="wkv_pool", bufs=8))
@@ -100,77 +100,101 @@ def tile_gemma3ntextattention_pa_k_kernel(
         position_int = keep.tile([P, 1], I32)
         nc.gpsimd.iota(position_int[:], pattern=[[0, 1]], base=0, channel_multiplier=1)
 
+        q_psum = ctx.enter_context(tc.psum_pool(name="q_psum", bufs=1, reuse_waits="tile"))
+        q_acc = [
+            [q_psum.tile([P, BANK], F32, name="q_acc_%d_%d" % (b, c)) for c in range(2)] for b in range(BATCH)
+        ]
 
         x_codes = keep.tile([P, BATCH, GROUPS, P], I32, align_bytes=64)
         x_planes = keep.tile([P, BATCH, GROUPS, P], U8, align_bytes=64)
 
-        def quantise(grouped, b, first_group):
-            groups = slice(first_group, first_group + X_GROUPS)
-            nc.vector.quantize_mx(
-                out=x_codes[:, b, groups, :].rearrange("p g m -> p (g m)").bitcast(FP8X4),
-                scales=x_planes[:, b, groups, :].rearrange("p g m -> p (g m)"),
-                in_=grouped[:].rearrange("p g m t -> p (g m t)"),
-            )
+        with tc.psum_pool(name="transposed", bufs=X_BANKS, reuse_waits="tile") as transposed:
 
-        with tc.psum_pool(name="transposed", bufs=2 * X_BANKS, reuse_waits="tile") as transposed:
-            waiting = None
-            for b in range(BATCH):
-                for first_group in range(0, GROUPS, X_GROUPS):
-                    x_rows = x_pool.tile([P, X_GROUPS * K_PASS], BF16)
-                    nc.sync.dma_start(
-                        out=x_rows[:],
-                        in_=hidden_states[
-                            b, :, first_group * K_PASS : (first_group + X_GROUPS) * K_PASS
-                        ],
+            def load_and_quantise_x(chunk, b):
+                first_group = chunk * X_GROUPS
+                groups = slice(first_group, first_group + X_GROUPS)
+                x_rows = x_pool.tile([P, X_GROUPS * K_PASS], BF16, name="x_rows")
+                nc.sync.dma_start(
+                    out=x_rows[:],
+                    in_=hidden_states[b, :, first_group * K_PASS : (first_group + X_GROUPS) * K_PASS],
+                )
+                x_words = x_rows[:].bitcast(F32)
+                grouped = grouped_pool.tile([P, X_GROUPS, P, 4], BF16, name="grouped", align_bytes=64)
+                for i in range(X_BANKS):
+                    bank = transposed.tile([P, BANK_GROUPS, 2, P], F32, name="bank")
+                    for j in range(BANK_GROUPS):
+                        start = (i * BANK_GROUPS + j) * (K_PASS // 2)
+                        for u in range(2):
+                            nc.tensor.transpose(
+                                bank[:, j, u, :],
+                                x_words[:, start + u : start + K_PASS // 2 : 2],
+                                identity[:],
+                            )
+                    target = (
+                        grouped[:, i * BANK_GROUPS : (i + 1) * BANK_GROUPS, :, :]
+                        .rearrange("p g m t -> p g (m t)")
+                        .bitcast(F32)
+                        .rearrange("p g (m u) -> p g m u", u=2)
                     )
-                    if b == 0 and first_group == 0:
-                        for row in range(16):
-                            load_scale_rows(nc, wq_planes, wq_scales, (row,))
-                            load_scale_rows(nc, wk_planes, wk_scales, (row,))
-                            load_scale_rows(nc, wv_planes, wv_scales, (row,))
-                    x_words = x_rows[:].bitcast(F32)
-                    banks = []
-                    for i in range(X_BANKS):
-                        bank = transposed.tile([P, BANK_GROUPS, 2, P], F32, name="bank")
-                        banks.append(bank)
-                        for j in range(BANK_GROUPS):
-                            start = (i * BANK_GROUPS + j) * (K_PASS // 2)
-                            for u in range(2):
-                                nc.tensor.transpose(
-                                    bank[:, j, u, :],
-                                    x_words[:, start + u : start + K_PASS // 2 : 2],
-                                    identity[:],
-                                )
-                    if waiting is not None:
-                        quantise(*waiting)
-                    grouped = grouped_pool.tile([P, X_GROUPS, P, 4], BF16, align_bytes=64)
-                    for i in range(X_BANKS):
-                        target = (
-                            grouped[:, i * BANK_GROUPS : (i + 1) * BANK_GROUPS, :, :]
-                            .rearrange("p g m t -> p g (m t)")
-                            .bitcast(F32)
-                            .rearrange("p g (m u) -> p g m u", u=2)
-                        )
-                        source = banks[i][:].rearrange("p g u m -> p g m u")
-                        if i == X_BANKS - 1:
-                            nc.vector.tensor_copy(out=target, in_=source)
-                        else:
-                            nc.scalar.copy(out=target, in_=source)
-                    waiting = (grouped, b, first_group)
-            quantise(*waiting)
+                    source = bank[:].rearrange("p g u m -> p g m u")
+                    if i == X_BANKS - 1:
+                        nc.vector.tensor_copy(out=target, in_=source)
+                    else:
+                        nc.scalar.copy(out=target, in_=source)
+                nc.vector.quantize_mx(
+                    out=x_codes[:, b, groups, :].rearrange("p g m -> p (g m)").bitcast(FP8X4),
+                    scales=x_planes[:, b, groups, :].rearrange("p g m -> p (g m)"),
+                    in_=grouped[:].rearrange("p g m t -> p (g m t)"),
+                )
 
-        with tc.psum_pool(name="sums_psum", bufs=1, reuse_waits="tile") as sums_psum:
-            q_acc = [
-                [sums_psum.tile([P, BANK], F32, name="q_acc_%d_%d" % (b, c)) for c in range(2)]
-                for b in range(BATCH)
-            ]
-            v_acc = [sums_psum.tile([P, BANK], F32, name="v_acc_%d" % b) for b in range(BATCH)]
-            k_acc = [sums_psum.tile([P, BANK], F32, name="k_acc_%d" % b) for b in range(BATCH)]
+            def multiply_q(first_group):
+                words = wq_pool.tile([P, WQ_GROUPS, Q_HEADS * HEAD], I32, name="wq_tile", align_bytes=64)
+                nc.sync.dma_start(
+                    out=words[:],
+                    in_=wq_words[first_group : first_group + WQ_GROUPS]
+                    .rearrange("g p n t -> p g (n t)")
+                    .bitcast(I32),
+                )
+                for j in range(WQ_GROUPS):
+                    g = first_group + j
+                    for b in range(BATCH):
+                        for c in range(2):
+                            columns = slice(c * BANK, (c + 1) * BANK)
+                            nc.tensor.matmul_mx(
+                                out=q_acc[b][c][:],
+                                lhsT=x_codes[:, b, g, :].bitcast(FP8X4),
+                                lhsT_scale=x_planes[:, b, g, :],
+                                rhs=words[:, j, columns].bitcast(FP8X4),
+                                rhs_scale=plane_of(wq_planes, g, columns),
+                                start=(g == 0),
+                                stop=(g == GROUPS - 1),
+                            )
 
-            gains = keep.tile([P, 2, 2, HALF], F32)
-            spare = v_acc[0][:, BANK - 2 * HEAD : BANK]
-            nc.tensor.matmul(out=spare, lhsT=ones[:], rhs=gain_rows[:], start=True, stop=True)
-            nc.vector.tensor_copy(out=gains[:].rearrange("p w h d -> p (w h d)"), in_=spare)
+            load_and_quantise_x(0, 0)
+            for row in range(16):
+                load_scale_rows(nc, wq_planes, wq_scales, (row,))
+                load_scale_rows(nc, wk_planes, wk_scales, (row,))
+                load_scale_rows(nc, wv_planes, wv_scales, (row,))
+            load_and_quantise_x(0, 1)
+
+            for chunk in range(GROUPS // X_GROUPS):
+                for i in range(X_GROUPS // WQ_GROUPS):
+                    multiply_q(chunk * X_GROUPS + i * WQ_GROUPS)
+                    if i < BATCH and chunk + 1 < GROUPS // X_GROUPS:
+                        load_and_quantise_x(chunk + 1, i)
+                if chunk == 0:
+                    gain_bank = transposed.tile([P, BANK], F32, name="bank")
+                    nc.tensor.matmul(
+                        out=gain_bank[:, 0 : 2 * HEAD], lhsT=ones[:], rhs=gain_rows[:], start=True, stop=True
+                    )
+                    gains = keep.tile([P, 2, 2, HALF], F32)
+                    nc.vector.tensor_copy(
+                        out=gains[:].rearrange("p w h d -> p (w h d)"), in_=gain_bank[:, 0 : 2 * HEAD]
+                    )
+
+        with tc.psum_pool(name="kv_psum", bufs=1, reuse_waits="tile") as kv_psum:
+            k_acc = [kv_psum.tile([P, BANK], F32, name="k_acc_%d" % b) for b in range(BATCH)]
+            v_acc = [kv_psum.tile([P, BANK], F32, name="v_acc_%d" % b) for b in range(BATCH)]
 
             inv_freq = keep.tile([P, HALF], F32)
             nc.vector.memset(inv_freq[:, 0:1], 1.0)
@@ -267,28 +291,6 @@ def tile_gemma3ntextattention_pa_k_kernel(
                 )
                 return turned
 
-            for first_group in range(0, GROUPS, WQ_GROUPS):
-                words = wq_pool.tile([P, WQ_GROUPS, Q_HEADS * HEAD], I32, name="wq_tile", align_bytes=64)
-                nc.sync.dma_start(
-                    out=words[:],
-                    in_=wq_words[first_group : first_group + WQ_GROUPS]
-                    .rearrange("g p n t -> p g (n t)")
-                    .bitcast(I32),
-                )
-                for j in range(WQ_GROUPS):
-                    g = first_group + j
-                    for b in range(BATCH):
-                        for c in range(2):
-                            columns = slice(c * BANK, (c + 1) * BANK)
-                            nc.tensor.matmul_mx(
-                                out=q_acc[b][c][:],
-                                lhsT=x_codes[:, b, g, :].bitcast(FP8X4),
-                                lhsT_scale=x_planes[:, b, g, :],
-                                rhs=words[:, j, columns].bitcast(FP8X4),
-                                rhs_scale=plane_of(wq_planes, g, columns),
-                                start=(g == 0),
-                                stop=(g == GROUPS - 1),
-                            )
             for b in range(BATCH):
                 for c in range(2):
                     result = rotated(normalised(q_acc[b][c], 4), 4, 0)

@@ -80,7 +80,7 @@ def tile_gemma3ntextattention_pa_k_kernel(
         grouped_pool = ctx.enter_context(tc.tile_pool(name="grouped_pool", bufs=2))
         wq_pool = ctx.enter_context(tc.tile_pool(name="wq_pool", bufs=5))
         wkv_pool = ctx.enter_context(tc.tile_pool(name="wkv_pool", bufs=8))
-        work = ctx.enter_context(tc.tile_pool(name="work", bufs=2))
+        work = ctx.enter_context(tc.tile_pool(name="work", bufs=4))
 
         wq_planes = keep.tile([P, SLOTS, Q_HEADS * HEAD], U8, align_bytes=64)
         wk_planes = keep.tile([P, SLOTS, KV_HEADS * HEAD], U8, align_bytes=64)
@@ -170,18 +170,24 @@ def tile_gemma3ntextattention_pa_k_kernel(
                                 stop=(g == GROUPS - 1),
                             )
 
-            load_and_quantise_x(0, 0)
-            for row in range(16):
-                load_scale_rows(nc, wq_planes, wq_scales, (row,))
-                load_scale_rows(nc, wk_planes, wk_scales, (row,))
-                load_scale_rows(nc, wv_planes, wv_scales, (row,))
-            load_and_quantise_x(0, 1)
+            scale_rows = [(wq_planes, wq_scales, row) for row in range(16)]
+            scale_rows += [(wk_planes, wk_scales, row) for row in range(16)]
+            scale_rows += [(wv_planes, wv_scales, row) for row in range(16)]
 
+            def load_scales(first, count):
+                for planes, scales, row in scale_rows[first : first + count]:
+                    load_scale_rows(nc, planes, scales, (row,))
+
+            for chunk in range(2):
+                for b in range(BATCH):
+                    load_and_quantise_x(chunk, b)
+                    load_scales(8 * chunk + 4 * b, 4)
             for chunk in range(GROUPS // X_GROUPS):
                 for i in range(X_GROUPS // WQ_GROUPS):
                     multiply_q(chunk * X_GROUPS + i * WQ_GROUPS)
-                    if i < BATCH and chunk + 1 < GROUPS // X_GROUPS:
-                        load_and_quantise_x(chunk + 1, i)
+                    load_scales(16 + 2 * (4 * chunk + i), 2)
+                    if i < BATCH and chunk + 2 < GROUPS // X_GROUPS:
+                        load_and_quantise_x(chunk + 2, i)
                 if chunk == 0:
                     gain_bank = transposed.tile([P, BANK], F32, name="bank")
                     nc.tensor.matmul(
@@ -232,6 +238,8 @@ def tile_gemma3ntextattention_pa_k_kernel(
             nc.scalar.activation(out=sin[:], in_=angle[:], func=ACT.Sin)
             cos = keep.tile([P, HALF], F32)
             nc.scalar.activation(out=cos[:], in_=angle_abs[:], func=ACT.Sin, bias=math.pi / 2.0, scale=-1.0)
+            sqrt_warm = keep.tile([P, 1], F32)
+            nc.scalar.activation(out=sqrt_warm[:], in_=position[:], func=ACT.Sqrt)
             same = keep.tile([P, 2, 2, HALF], F32)
             other = keep.tile([P, 2, 2, HALF], F32)
             for w in range(2):
@@ -324,7 +332,7 @@ def tile_gemma3ntextattention_pa_k_kernel(
                 if acc is k_acc:
                     for b in range(BATCH):
                         result = rotated(normalised(k_acc[b], KV_HEADS), KV_HEADS, 1)
-                        nc.gpsimd.dma_start(
+                        nc.scalar.dma_start(
                             out=out_1[b].rearrange("s h d -> s (h d)"),
                             in_=result[:, 0:KV_HEADS, :, :].rearrange("p h s d -> p (h s d)"),
                         )

@@ -34,6 +34,7 @@ WKV_GROUPS = 4
 
 PLANES = 4
 SLOTS = GROUPS // PLANES
+COLUMNS = (Q_HEADS + 2 * KV_HEADS) * HEAD
 
 FLOPS = 2 * BATCH * P * HIDDEN * (Q_HEADS + 2 * KV_HEADS) * HEAD
 
@@ -43,13 +44,17 @@ TWO_PI_LOW = 2.0 * math.pi - TWO_PI_HIGH - TWO_PI_MID
 ROUND_TO_WHOLE = 12582912.0
 
 
-def load_scale_rows(nc, planes, scales, rows):
-    by_row = scales.rearrange("(j k) q n -> q k j n", k=PLANES)
-    for row in rows:
-        first = 32 * (row // 4) + row % 4
+def stage_scales(nc, stage, scales, columns):
+    by_r = scales.rearrange("g (q r) n -> r g q n", r=4)
+    for r in range(4):
+        nc.sync.dma_start(out=stage[r:P:4, :, columns].bitcast(I32), in_=by_r[r].bitcast(I32))
+
+
+def place_scales(nc, planes, stage, slot):
+    for quadrant in (0, 2, 1, 3):
         nc.sync.dma_start(
-            out=planes[first : first + 4 * PLANES : 4, :, :].bitcast(I32),
-            in_=by_row[row].bitcast(I32),
+            out=planes[32 * quadrant : 32 * quadrant + 16, slot, :].bitcast(I32),
+            in_=stage[16 * slot : 16 * slot + 16, quadrant, :].bitcast(I32),
         )
 
 
@@ -82,11 +87,12 @@ def tile_gemma3ntextattention_pa_k_kernel(
         wkv_pool = ctx.enter_context(tc.tile_pool(name="wkv_pool", bufs=8))
         work = ctx.enter_context(tc.tile_pool(name="work", bufs=4))
 
-        wq_planes = keep.tile([P, SLOTS, Q_HEADS * HEAD], U8, align_bytes=64)
-        wk_planes = keep.tile([P, SLOTS, KV_HEADS * HEAD], U8, align_bytes=64)
-        wv_planes = keep.tile([P, SLOTS, KV_HEADS * HEAD], U8, align_bytes=64)
-        for planes in (wq_planes, wk_planes, wv_planes):
-            nc.vector.memset(planes[:].rearrange("p j n -> p (j n)").bitcast(I32), 0)
+        q_columns = slice(0, Q_HEADS * HEAD)
+        k_columns = slice(Q_HEADS * HEAD, (Q_HEADS + KV_HEADS) * HEAD)
+        v_columns = slice((Q_HEADS + KV_HEADS) * HEAD, COLUMNS)
+        planes = keep.tile([P, SLOTS, COLUMNS], U8, align_bytes=64)
+        nc.vector.memset(planes[:].rearrange("p j n -> p (j n)").bitcast(I32), 0)
+        stage = keep.tile([P, 4, COLUMNS], U8, align_bytes=64)
 
         gain_rows = keep.tile([P, 2 * HEAD], BF16)
         nc.vector.memset(gain_rows[:], 0.0)
@@ -165,27 +171,27 @@ def tile_gemma3ntextattention_pa_k_kernel(
                                 lhsT=x_codes[:, b, g, :].bitcast(FP8X4),
                                 lhsT_scale=x_planes[:, b, g, :],
                                 rhs=words[:, j, columns].bitcast(FP8X4),
-                                rhs_scale=plane_of(wq_planes, g, columns),
+                                rhs_scale=plane_of(planes, g, columns),
                                 start=(g == 0),
                                 stop=(g == GROUPS - 1),
                             )
 
-            scale_rows = [(wq_planes, wq_scales, row) for row in range(16)]
-            scale_rows += [(wk_planes, wk_scales, row) for row in range(16)]
-            scale_rows += [(wv_planes, wv_scales, row) for row in range(16)]
-
-            def load_scales(first, count):
-                for planes, scales, row in scale_rows[first : first + count]:
-                    load_scale_rows(nc, planes, scales, (row,))
-
-            for chunk in range(2):
-                for b in range(BATCH):
-                    load_and_quantise_x(chunk, b)
-                    load_scales(8 * chunk + 4 * b, 4)
+            load_and_quantise_x(0, 0)
+            stage_scales(nc, stage, wq_scales, q_columns)
+            stage_scales(nc, stage, wk_scales, k_columns)
+            stage_scales(nc, stage, wv_scales, v_columns)
+            load_and_quantise_x(0, 1)
+            load_and_quantise_x(1, 0)
+            place_scales(nc, planes, stage, 0)
+            place_scales(nc, planes, stage, 1)
+            load_and_quantise_x(1, 1)
+            place_scales(nc, planes, stage, 2)
+            place_scales(nc, planes, stage, 3)
             for chunk in range(GROUPS // X_GROUPS):
                 for i in range(X_GROUPS // WQ_GROUPS):
                     multiply_q(chunk * X_GROUPS + i * WQ_GROUPS)
-                    load_scales(16 + 2 * (4 * chunk + i), 2)
+                    if chunk == 0:
+                        place_scales(nc, planes, stage, 4 + i)
                     if i < BATCH and chunk + 2 < GROUPS // X_GROUPS:
                         load_and_quantise_x(chunk + 2, i)
                 if chunk == 0:
@@ -308,7 +314,7 @@ def tile_gemma3ntextattention_pa_k_kernel(
                     )
 
             kv_width = KV_HEADS * HEAD
-            for w_words, planes, acc in ((wk_words, wk_planes, k_acc), (wv_words, wv_planes, v_acc)):
+            for w_words, columns, acc in ((wk_words, k_columns, k_acc), (wv_words, v_columns, v_acc)):
                 for first_group in range(0, GROUPS, WKV_GROUPS):
                     words = wkv_pool.tile([P, WKV_GROUPS, kv_width], I32, name="wkv_tile", align_bytes=64)
                     nc.sync.dma_start(
@@ -325,7 +331,7 @@ def tile_gemma3ntextattention_pa_k_kernel(
                                 lhsT=x_codes[:, b, g, :].bitcast(FP8X4),
                                 lhsT_scale=x_planes[:, b, g, :],
                                 rhs=words[:, j, :].bitcast(FP8X4),
-                                rhs_scale=plane_of(planes, g, slice(0, kv_width)),
+                                rhs_scale=plane_of(planes, g, columns),
                                 start=(g == 0),
                                 stop=(g == GROUPS - 1),
                             )

@@ -29,8 +29,9 @@ BANK = 512
 X_GROUPS = 8
 BANK_GROUPS = 2
 X_BANKS = X_GROUPS // BANK_GROUPS
-WQ_GROUPS = 2
-WKV_GROUPS = 4
+WQ_GROUPS = 4
+WK_LOADS = (8, 8, 8, 8)
+WV_LOADS = (8, 8, 8, 4, 2, 1, 1)
 
 PLANES = 4
 SLOTS = GROUPS // PLANES
@@ -50,8 +51,8 @@ def stage_scales(nc, stage, scales, columns):
         nc.sync.dma_start(out=stage[r:P:4, :, columns].bitcast(I32), in_=by_r[r].bitcast(I32))
 
 
-def place_scales(nc, planes, stage, slot):
-    for quadrant in (0, 2, 1, 3):
+def place_scales(nc, planes, stage, slot, quadrants):
+    for quadrant in quadrants:
         nc.sync.dma_start(
             out=planes[32 * quadrant : 32 * quadrant + 16, slot, :].bitcast(I32),
             in_=stage[16 * slot : 16 * slot + 16, quadrant, :].bitcast(I32),
@@ -83,9 +84,10 @@ def tile_gemma3ntextattention_pa_k_kernel(
         keep = ctx.enter_context(tc.tile_pool(name="keep", bufs=1))
         x_pool = ctx.enter_context(tc.tile_pool(name="x_pool", bufs=4))
         grouped_pool = ctx.enter_context(tc.tile_pool(name="grouped_pool", bufs=2))
-        wq_pool = ctx.enter_context(tc.tile_pool(name="wq_pool", bufs=5))
-        wkv_pool = ctx.enter_context(tc.tile_pool(name="wkv_pool", bufs=8))
+        wq_pool = ctx.enter_context(tc.tile_pool(name="wq_pool", bufs=3))
+        wkv_pool = ctx.enter_context(tc.tile_pool(name="wkv_pool", bufs=5))
         work = ctx.enter_context(tc.tile_pool(name="work", bufs=4))
+        junk = ctx.enter_context(tc.tile_pool(name="junk", bufs=1))
 
         q_columns = slice(0, Q_HEADS * HEAD)
         k_columns = slice(Q_HEADS * HEAD, (Q_HEADS + KV_HEADS) * HEAD)
@@ -178,21 +180,20 @@ def tile_gemma3ntextattention_pa_k_kernel(
 
             load_and_quantise_x(0, 0)
             stage_scales(nc, stage, wq_scales, q_columns)
+            load_and_quantise_x(0, 1)
             stage_scales(nc, stage, wk_scales, k_columns)
             stage_scales(nc, stage, wv_scales, v_columns)
-            load_and_quantise_x(0, 1)
             load_and_quantise_x(1, 0)
-            place_scales(nc, planes, stage, 0)
-            place_scales(nc, planes, stage, 1)
+            place_scales(nc, planes, stage, 0, (0, 2))
             load_and_quantise_x(1, 1)
-            place_scales(nc, planes, stage, 2)
-            place_scales(nc, planes, stage, 3)
+            place_scales(nc, planes, stage, 0, (1, 3))
             for chunk in range(GROUPS // X_GROUPS):
                 for i in range(X_GROUPS // WQ_GROUPS):
-                    multiply_q(chunk * X_GROUPS + i * WQ_GROUPS)
-                    if chunk == 0:
-                        place_scales(nc, planes, stage, 4 + i)
-                    if i < BATCH and chunk + 2 < GROUPS // X_GROUPS:
+                    slot = chunk * X_GROUPS // WQ_GROUPS + i
+                    multiply_q(slot * WQ_GROUPS)
+                    if slot + 1 < SLOTS:
+                        place_scales(nc, planes, stage, slot + 1, (0, 2, 1, 3))
+                    if chunk + 2 < GROUPS // X_GROUPS:
                         load_and_quantise_x(chunk + 2, i)
                 if chunk == 0:
                     gain_bank = transposed.tile([P, BANK], F32, name="bank")
@@ -261,7 +262,7 @@ def tile_gemma3ntextattention_pa_k_kernel(
                 nc.vector.tensor_tensor(out=other[:, w, 1, :], in0=gains[:, w, 0, :], in1=sin[:], op=ALU.mult)
 
             def normalised(acc, heads):
-                squares = work.tile([P, BANK], F32, name="squares")
+                squares = junk.tile([P, BANK], F32, name="squares")
                 sums = work.tile([P, 4], F32, name="sums")
                 for h in range(heads):
                     columns = slice(h * HEAD, (h + 1) * HEAD)
@@ -314,17 +315,21 @@ def tile_gemma3ntextattention_pa_k_kernel(
                     )
 
             kv_width = KV_HEADS * HEAD
-            for w_words, columns, acc in ((wk_words, k_columns, k_acc), (wv_words, v_columns, v_acc)):
-                for first_group in range(0, GROUPS, WKV_GROUPS):
-                    words = wkv_pool.tile([P, WKV_GROUPS, kv_width], I32, name="wkv_tile", align_bytes=64)
+            for w_words, columns, acc, loads in (
+                (wk_words, k_columns, k_acc, WK_LOADS),
+                (wv_words, v_columns, v_acc, WV_LOADS),
+            ):
+                for n, count in enumerate(loads):
+                    first_group = sum(loads[:n])
+                    words = wkv_pool.tile([P, count, kv_width], I32, name="wkv_tile", align_bytes=64)
                     nc.sync.dma_start(
                         out=words[:],
-                        in_=w_words[first_group : first_group + WKV_GROUPS]
+                        in_=w_words[first_group : first_group + count]
                         .rearrange("g p n t -> p g (n t)")
                         .bitcast(I32),
                     )
                     for b in range(BATCH):
-                        for j in range(WKV_GROUPS):
+                        for j in range(count):
                             g = first_group + j
                             nc.tensor.matmul_mx(
                                 out=acc[b][:, 0:kv_width],

@@ -82,11 +82,12 @@ def tile_gemma3ntextattention_pa_k_kernel(
     with ExitStack() as ctx:
         ctx.enter_context(tc.manual_schedule())
         keep = ctx.enter_context(tc.tile_pool(name="keep", bufs=1))
-        x_pool = ctx.enter_context(tc.tile_pool(name="x_pool", bufs=4))
+        x_pool = ctx.enter_context(tc.tile_pool(name="x_pool", bufs=3))
+        split_pool = ctx.enter_context(tc.tile_pool(name="split_pool", bufs=2))
         grouped_pool = ctx.enter_context(tc.tile_pool(name="grouped_pool", bufs=2))
         wq_pool = ctx.enter_context(tc.tile_pool(name="wq_pool", bufs=3))
         wkv_pool = ctx.enter_context(tc.tile_pool(name="wkv_pool", bufs=5))
-        work = ctx.enter_context(tc.tile_pool(name="work", bufs=4))
+        work = ctx.enter_context(tc.tile_pool(name="work", bufs=3))
         junk = ctx.enter_context(tc.tile_pool(name="junk", bufs=1))
 
         q_columns = slice(0, Q_HEADS * HEAD)
@@ -118,25 +119,28 @@ def tile_gemma3ntextattention_pa_k_kernel(
 
         with tc.psum_pool(name="transposed", bufs=X_BANKS, reuse_waits="tile") as transposed:
 
-            def load_and_quantise_x(chunk, b):
+            def load_x(chunk, b):
                 first_group = chunk * X_GROUPS
-                groups = slice(first_group, first_group + X_GROUPS)
                 x_rows = x_pool.tile([P, X_GROUPS * K_PASS], BF16, name="x_rows")
                 nc.sync.dma_start(
                     out=x_rows[:],
                     in_=hidden_states[b, :, first_group * K_PASS : (first_group + X_GROUPS) * K_PASS],
                 )
-                x_words = x_rows[:].bitcast(F32)
+                parted = split_pool.tile([P, X_GROUPS, 2, P], F32, name="parted")
+                nc.vector.tensor_copy(
+                    out=parted[:], in_=x_rows[:].bitcast(F32).rearrange("p (g w u) -> p g u w", w=P, u=2)
+                )
+                return parted
+
+            def quantise_x(parted, chunk, b):
+                groups = slice(chunk * X_GROUPS, (chunk + 1) * X_GROUPS)
                 grouped = grouped_pool.tile([P, X_GROUPS, P, 4], BF16, name="grouped", align_bytes=64)
                 for i in range(X_BANKS):
                     bank = transposed.tile([P, BANK_GROUPS, 2, P], F32, name="bank")
                     for j in range(BANK_GROUPS):
-                        start = (i * BANK_GROUPS + j) * (K_PASS // 2)
                         for u in range(2):
                             nc.tensor.transpose(
-                                bank[:, j, u, :],
-                                x_words[:, start + u : start + K_PASS // 2 : 2],
-                                identity[:],
+                                bank[:, j, u, :], parted[:, i * BANK_GROUPS + j, u, :], identity[:]
                             )
                     target = (
                         grouped[:, i * BANK_GROUPS : (i + 1) * BANK_GROUPS, :, :]
@@ -178,24 +182,29 @@ def tile_gemma3ntextattention_pa_k_kernel(
                                 stop=(g == GROUPS - 1),
                             )
 
-            load_and_quantise_x(0, 0)
+            x_loads = [(chunk, b) for chunk in range(GROUPS // X_GROUPS) for b in range(BATCH)]
+            parted = load_x(*x_loads[0])
             stage_scales(nc, stage, wq_scales, q_columns)
-            load_and_quantise_x(0, 1)
+            parted_next = load_x(*x_loads[1])
+            quantise_x(parted, *x_loads[0])
             stage_scales(nc, stage, wk_scales, k_columns)
             stage_scales(nc, stage, wv_scales, v_columns)
-            load_and_quantise_x(1, 0)
+            parted = load_x(*x_loads[2])
+            quantise_x(parted_next, *x_loads[1])
             place_scales(nc, planes, stage, 0, (0, 2))
-            load_and_quantise_x(1, 1)
+            parted_next = load_x(*x_loads[3])
+            quantise_x(parted, *x_loads[2])
             place_scales(nc, planes, stage, 0, (1, 3))
-            for chunk in range(GROUPS // X_GROUPS):
-                for i in range(X_GROUPS // WQ_GROUPS):
-                    slot = chunk * X_GROUPS // WQ_GROUPS + i
-                    multiply_q(slot * WQ_GROUPS)
-                    if slot + 1 < SLOTS:
-                        place_scales(nc, planes, stage, slot + 1, (0, 2, 1, 3))
-                    if chunk + 2 < GROUPS // X_GROUPS:
-                        load_and_quantise_x(chunk + 2, i)
-                if chunk == 0:
+            for slot in range(SLOTS):
+                multiply_q(slot * WQ_GROUPS)
+                if slot + 1 < SLOTS:
+                    place_scales(nc, planes, stage, slot + 1, (0, 2, 1, 3))
+                parted = parted_next
+                if slot + 4 < len(x_loads):
+                    parted_next = load_x(*x_loads[slot + 4])
+                if slot + 3 < len(x_loads):
+                    quantise_x(parted, *x_loads[slot + 3])
+                if slot == 1:
                     gain_bank = transposed.tile([P, BANK], F32, name="bank")
                     nc.tensor.matmul(
                         out=gain_bank[:, 0 : 2 * HEAD], lhsT=ones[:], rhs=gain_rows[:], start=True, stop=True
@@ -261,7 +270,7 @@ def tile_gemma3ntextattention_pa_k_kernel(
                 )
                 nc.vector.tensor_tensor(out=other[:, w, 1, :], in0=gains[:, w, 0, :], in1=sin[:], op=ALU.mult)
 
-            def normalised(acc, heads):
+            def root_mean_squares(acc, heads):
                 squares = junk.tile([P, BANK], F32, name="squares")
                 sums = work.tile([P, 4], F32, name="sums")
                 for h in range(heads):
@@ -273,24 +282,21 @@ def tile_gemma3ntextattention_pa_k_kernel(
                 nc.scalar.activation(
                     out=rms[:, 0:heads], in_=sums[:, 0:heads], func=ACT.Sqrt, bias=EPS, scale=1.0 / HEAD
                 )
+                return rms
+
+            def inverted(rms, heads):
                 inverse = work.tile([P, 4], F32, name="inverse")
                 nc.vector.reciprocal(out=inverse[:, 0:heads], in_=rms[:, 0:heads])
-                unit = work.tile([P, 4, HEAD], F32, name="unit")
-                nc.vector.tensor_tensor(
-                    out=unit[:, 0:heads, :],
-                    in0=acc[:, 0 : heads * HEAD].rearrange("p (h d) -> p h d", d=HEAD),
-                    in1=inverse[:, 0:heads].unsqueeze(2).to_broadcast([P, heads, HEAD]),
-                    op=ALU.mult,
-                )
-                return unit
+                return inverse
 
-            def rotated(unit, heads, w):
-                halves = unit[:, 0:heads, :].rearrange("p h (s d) -> p h s d", s=2)
+            def rotated(acc, heads, w):
+                sums = acc[:, 0 : heads * HEAD].rearrange("p (h d) -> p h d", d=HEAD)
+                halves = acc[:, 0 : heads * HEAD].rearrange("p (h s d) -> p h s d", s=2, d=HALF)
                 turned = work.tile([P, 4, 2, HALF], F32, name="turned")
                 crossed = work.tile([P, 4, 2, HALF], F32, name="crossed")
                 nc.vector.tensor_tensor(
                     out=turned[:, 0:heads, :, :].rearrange("p h s d -> p h (s d)"),
-                    in0=unit[:, 0:heads, :],
+                    in0=sums,
                     in1=same[:, w, :, :].rearrange("p s d -> p (s d)").unsqueeze(1).to_broadcast([P, heads, HEAD]),
                     op=ALU.mult,
                 )
@@ -306,13 +312,33 @@ def tile_gemma3ntextattention_pa_k_kernel(
                 )
                 return turned
 
+            def scaled(turned, inverse, heads):
+                result = work.tile([P, 4, HEAD], F32, name="result")
+                for h in range(heads):
+                    nc.scalar.activation(
+                        out=result[:, h, :],
+                        in_=turned[:, h, :, :].rearrange("p s d -> p (s d)"),
+                        func=ACT.Copy,
+                        scale=inverse[:, h : h + 1],
+                    )
+                return result
+
+            def store_q(turned, inverse, b, c):
+                result = scaled(turned, inverse, 4)
+                nc.gpsimd.dma_start(
+                    out=out_0[b, :, 4 * c : 4 * c + 4, :].rearrange("s h d -> s (h d)"),
+                    in_=result[:].rearrange("p h d -> p (h d)"),
+                )
+
+            waiting = None
             for b in range(BATCH):
                 for c in range(2):
-                    result = rotated(normalised(q_acc[b][c], 4), 4, 0)
-                    nc.gpsimd.dma_start(
-                        out=out_0[b, :, 4 * c : 4 * c + 4, :].rearrange("s h d -> s (h d)"),
-                        in_=result[:].rearrange("p h s d -> p (h s d)"),
-                    )
+                    rms = root_mean_squares(q_acc[b][c], 4)
+                    turned = rotated(q_acc[b][c], 4, 0)
+                    if waiting is not None:
+                        store_q(*waiting)
+                    waiting = (turned, inverted(rms, 4), b, c)
+            store_q(*waiting)
 
             kv_width = KV_HEADS * HEAD
             for w_words, columns, acc, loads in (
@@ -341,15 +367,25 @@ def tile_gemma3ntextattention_pa_k_kernel(
                                 stop=(g == GROUPS - 1),
                             )
                 if acc is k_acc:
-                    for b in range(BATCH):
-                        result = rotated(normalised(k_acc[b], KV_HEADS), KV_HEADS, 1)
-                        nc.scalar.dma_start(
-                            out=out_1[b].rearrange("s h d -> s (h d)"),
-                            in_=result[:, 0:KV_HEADS, :, :].rearrange("p h s d -> p (h s d)"),
-                        )
+                    steps = [
+                        (root_mean_squares(k_acc[b], KV_HEADS), rotated(k_acc[b], KV_HEADS, 1)) for b in range(BATCH)
+                    ]
+                    k_results = [scaled(turned, inverted(rms, KV_HEADS), KV_HEADS) for rms, turned in steps]
             for b in range(BATCH):
-                result = normalised(v_acc[b], KV_HEADS)
+                nc.sync.dma_start(
+                    out=out_1[b].rearrange("s h d -> s (h d)"),
+                    in_=k_results[b][:, 0:KV_HEADS, :].rearrange("p h d -> p (h d)"),
+                )
+            for b in range(BATCH):
+                inverse = inverted(root_mean_squares(v_acc[b], KV_HEADS), KV_HEADS)
+                result = work.tile([P, KV_HEADS, HEAD], F32, name="v_result")
+                nc.vector.tensor_tensor(
+                    out=result[:],
+                    in0=v_acc[b][:, 0 : KV_HEADS * HEAD].rearrange("p (h d) -> p h d", d=HEAD),
+                    in1=inverse[:, 0:KV_HEADS].unsqueeze(2).to_broadcast([P, KV_HEADS, HEAD]),
+                    op=ALU.mult,
+                )
                 nc.sync.dma_start(
                     out=out_2[b].rearrange("s h d -> s (h d)"),
-                    in_=result[:, 0:KV_HEADS, :].rearrange("p h d -> p (h d)"),
+                    in_=result[:].rearrange("p h d -> p (h d)"),
                 )

@@ -86,7 +86,7 @@ def tile_gemma3ntextattention_pa_k_kernel(
         split_pool = ctx.enter_context(tc.tile_pool(name="split_pool", bufs=2))
         grouped_pool = ctx.enter_context(tc.tile_pool(name="grouped_pool", bufs=2))
         wq_pool = ctx.enter_context(tc.tile_pool(name="wq_pool", bufs=3))
-        wkv_pool = ctx.enter_context(tc.tile_pool(name="wkv_pool", bufs=5))
+        wkv_pool = ctx.enter_context(tc.tile_pool(name="wkv_pool", bufs=4))
         work = ctx.enter_context(tc.tile_pool(name="work", bufs=3))
         junk = ctx.enter_context(tc.tile_pool(name="junk", bufs=1))
 
@@ -101,8 +101,8 @@ def tile_gemma3ntextattention_pa_k_kernel(
         nc.vector.memset(gain_rows[:], 0.0)
         ones = keep.tile([P, P], BF16)
         nc.vector.memset(ones[:], 1.0)
-        nc.scalar.dma_start(out=gain_rows[0:1, 0:HEAD], in_=q_scale.unsqueeze(0))
-        nc.scalar.dma_start(out=gain_rows[0:1, HEAD : 2 * HEAD], in_=k_scale.unsqueeze(0))
+        nc.gpsimd.dma_start(out=gain_rows[0:1, 0:HEAD], in_=q_scale.unsqueeze(0))
+        nc.gpsimd.dma_start(out=gain_rows[0:1, HEAD : 2 * HEAD], in_=k_scale.unsqueeze(0))
 
         identity = keep.tile([P, P], F32)
         make_identity(nc, identity[:])
@@ -159,7 +159,8 @@ def tile_gemma3ntextattention_pa_k_kernel(
                     in_=grouped[:].rearrange("p g m t -> p (g m t)"),
                 )
 
-            def multiply_q(first_group):
+            def load_wq(slot):
+                first_group = slot * WQ_GROUPS
                 words = wq_pool.tile([P, WQ_GROUPS, Q_HEADS * HEAD], I32, name="wq_tile", align_bytes=64)
                 nc.sync.dma_start(
                     out=words[:],
@@ -167,8 +168,11 @@ def tile_gemma3ntextattention_pa_k_kernel(
                     .rearrange("g p n t -> p g (n t)")
                     .bitcast(I32),
                 )
+                return words
+
+            def multiply_q(words, slot):
                 for j in range(WQ_GROUPS):
-                    g = first_group + j
+                    g = slot * WQ_GROUPS + j
                     for b in range(BATCH):
                         for c in range(2):
                             columns = slice(c * BANK, (c + 1) * BANK)
@@ -183,27 +187,24 @@ def tile_gemma3ntextattention_pa_k_kernel(
                             )
 
             x_loads = [(chunk, b) for chunk in range(GROUPS // X_GROUPS) for b in range(BATCH)]
-            parted = load_x(*x_loads[0])
+            first = load_x(*x_loads[0])
             stage_scales(nc, stage, wq_scales, q_columns)
-            parted_next = load_x(*x_loads[1])
-            quantise_x(parted, *x_loads[0])
+            second = load_x(*x_loads[1])
+            quantise_x(first, *x_loads[0])
             stage_scales(nc, stage, wk_scales, k_columns)
+            third = load_x(*x_loads[2])
+            quantise_x(second, *x_loads[1])
             stage_scales(nc, stage, wv_scales, v_columns)
-            parted = load_x(*x_loads[2])
-            quantise_x(parted_next, *x_loads[1])
-            place_scales(nc, planes, stage, 0, (0, 2))
-            parted_next = load_x(*x_loads[3])
-            quantise_x(parted, *x_loads[2])
-            place_scales(nc, planes, stage, 0, (1, 3))
+            quantise_x(third, *x_loads[2])
             for slot in range(SLOTS):
-                multiply_q(slot * WQ_GROUPS)
+                words = load_wq(slot)
+                if slot == 0:
+                    place_scales(nc, planes, stage, 0, (0, 2, 1, 3))
+                multiply_q(words, slot)
+                if slot + 3 < len(x_loads):
+                    quantise_x(load_x(*x_loads[slot + 3]), *x_loads[slot + 3])
                 if slot + 1 < SLOTS:
                     place_scales(nc, planes, stage, slot + 1, (0, 2, 1, 3))
-                parted = parted_next
-                if slot + 4 < len(x_loads):
-                    parted_next = load_x(*x_loads[slot + 4])
-                if slot + 3 < len(x_loads):
-                    quantise_x(parted, *x_loads[slot + 3])
                 if slot == 1:
                     gain_bank = transposed.tile([P, BANK], F32, name="bank")
                     nc.tensor.matmul(
@@ -312,8 +313,7 @@ def tile_gemma3ntextattention_pa_k_kernel(
                 )
                 return turned
 
-            def scaled(turned, inverse, heads):
-                result = work.tile([P, 4, HEAD], F32, name="result")
+            def scale_heads(result, turned, inverse, heads):
                 for h in range(heads):
                     nc.scalar.activation(
                         out=result[:, h, :],
@@ -321,24 +321,19 @@ def tile_gemma3ntextattention_pa_k_kernel(
                         func=ACT.Copy,
                         scale=inverse[:, h : h + 1],
                     )
-                return result
 
-            def store_q(turned, inverse, b, c):
-                result = scaled(turned, inverse, 4)
-                nc.gpsimd.dma_start(
-                    out=out_0[b, :, 4 * c : 4 * c + 4, :].rearrange("s h d -> s (h d)"),
-                    in_=result[:].rearrange("p h d -> p (h d)"),
-                )
-
+            q_results = keep.tile([P, BATCH, Q_HEADS, HEAD], F32)
+            k_results = keep.tile([P, BATCH, KV_HEADS, HEAD], F32)
+            v_results = keep.tile([P, BATCH, KV_HEADS, HEAD], F32)
             waiting = None
             for b in range(BATCH):
                 for c in range(2):
                     rms = root_mean_squares(q_acc[b][c], 4)
                     turned = rotated(q_acc[b][c], 4, 0)
                     if waiting is not None:
-                        store_q(*waiting)
-                    waiting = (turned, inverted(rms, 4), b, c)
-            store_q(*waiting)
+                        scale_heads(*waiting)
+                    waiting = (q_results[:, b, 4 * c : 4 * c + 4, :], turned, inverted(rms, 4), 4)
+            scale_heads(*waiting)
 
             kv_width = KV_HEADS * HEAD
             for w_words, columns, acc, loads in (
@@ -347,7 +342,10 @@ def tile_gemma3ntextattention_pa_k_kernel(
             ):
                 for n, count in enumerate(loads):
                     first_group = sum(loads[:n])
-                    words = wkv_pool.tile([P, count, kv_width], I32, name="wkv_tile", align_bytes=64)
+                    if count == WK_LOADS[0]:
+                        words = wkv_pool.tile([P, count, kv_width], I32, name="wkv_tile", align_bytes=64)
+                    else:
+                        words = keep.tile([P, count, kv_width], I32, name="wv_tile_%d" % n, align_bytes=64)
                     nc.sync.dma_start(
                         out=words[:],
                         in_=w_words[first_group : first_group + count]
@@ -370,22 +368,18 @@ def tile_gemma3ntextattention_pa_k_kernel(
                     steps = [
                         (root_mean_squares(k_acc[b], KV_HEADS), rotated(k_acc[b], KV_HEADS, 1)) for b in range(BATCH)
                     ]
-                    k_results = [scaled(turned, inverted(rms, KV_HEADS), KV_HEADS) for rms, turned in steps]
+                    for b, (rms, turned) in enumerate(steps):
+                        scale_heads(k_results[:, b, :, :], turned, inverted(rms, KV_HEADS), KV_HEADS)
             for b in range(BATCH):
-                nc.sync.dma_start(
-                    out=out_1[b].rearrange("s h d -> s (h d)"),
-                    in_=k_results[b][:, 0:KV_HEADS, :].rearrange("p h d -> p (h d)"),
-                )
+                nc.sync.dma_start(out=out_0[b], in_=q_results[:, b, :, :])
+            for b in range(BATCH):
+                nc.sync.dma_start(out=out_1[b], in_=k_results[:, b, :, :])
             for b in range(BATCH):
                 inverse = inverted(root_mean_squares(v_acc[b], KV_HEADS), KV_HEADS)
-                result = work.tile([P, KV_HEADS, HEAD], F32, name="v_result")
                 nc.vector.tensor_tensor(
-                    out=result[:],
+                    out=v_results[:, b, :, :],
                     in0=v_acc[b][:, 0 : KV_HEADS * HEAD].rearrange("p (h d) -> p h d", d=HEAD),
                     in1=inverse[:, 0:KV_HEADS].unsqueeze(2).to_broadcast([P, KV_HEADS, HEAD]),
                     op=ALU.mult,
                 )
-                nc.sync.dma_start(
-                    out=out_2[b].rearrange("s h d -> s (h d)"),
-                    in_=result[:].rearrange("p h d -> p (h d)"),
-                )
+                nc.sync.dma_start(out=out_2[b], in_=v_results[:, b, :, :])

import math
from contextlib import ExitStack

import concourse.mybir as mybir
from concourse.masks import make_identity

F32 = mybir.dt.float32
BF16 = mybir.dt.bfloat16
I32 = mybir.dt.int32
U8 = mybir.dt.uint8
FP8X4 = mybir.dt.float8_e4m3fn_x4
ALU = mybir.AluOpType
ACT = mybir.ActivationFunctionType

P = 128
BATCH = 2
HIDDEN = 16384
HEAD = 128
HALF = HEAD // 2
Q_HEADS = 8
KV_HEADS = 2
EPS = 1e-6
WAVELENGTH = 10000.0

K_PASS = 512
GROUPS = HIDDEN // K_PASS
BANK = 512

X_GROUPS = 8
BANK_GROUPS = 2
X_BANKS = X_GROUPS // BANK_GROUPS
WQ_GROUPS = 4
WK_LOADS = (8, 8, 8, 8)
WV_LOADS = (8, 8, 8, 4, 2, 1, 1)

PLANES = 4
SLOTS = GROUPS // PLANES
COLUMNS = (Q_HEADS + 2 * KV_HEADS) * HEAD

FLOPS = 2 * BATCH * P * HIDDEN * (Q_HEADS + 2 * KV_HEADS) * HEAD

TWO_PI_HIGH = 6.28125
TWO_PI_MID = 0.0019350051879882812
TWO_PI_LOW = 2.0 * math.pi - TWO_PI_HIGH - TWO_PI_MID
ROUND_TO_WHOLE = 12582912.0


def stage_scales(nc, stage, scales, columns):
    by_r = scales.rearrange("g (q r) n -> r g q n", r=4)
    for r in range(4):
        nc.sync.dma_start(out=stage[r:P:4, :, columns].bitcast(I32), in_=by_r[r].bitcast(I32))


def place_scales(nc, planes, stage, slot, quadrants):
    for quadrant in quadrants:
        nc.sync.dma_start(
            out=planes[32 * quadrant : 32 * quadrant + 16, slot, :].bitcast(I32),
            in_=stage[16 * slot : 16 * slot + 16, quadrant, :].bitcast(I32),
        )


def plane_of(planes, group, columns):
    return planes[4 * (group % PLANES) : P, group // PLANES, columns]


def tile_gemma3ntextattention_pa_k_kernel(
    tc,
    hidden_states,
    wq_words,
    wq_scales,
    wk_words,
    wk_scales,
    wv_words,
    wv_scales,
    q_scale,
    k_scale,
    out_0,
    out_1,
    out_2,
):
    nc = tc.nc
    with ExitStack() as ctx:
        ctx.enter_context(tc.manual_schedule())
        keep = ctx.enter_context(tc.tile_pool(name="keep", bufs=1))
        x_pool = ctx.enter_context(tc.tile_pool(name="x_pool", bufs=3))
        split_pool = ctx.enter_context(tc.tile_pool(name="split_pool", bufs=2))
        grouped_pool = ctx.enter_context(tc.tile_pool(name="grouped_pool", bufs=2))
        wq_pool = ctx.enter_context(tc.tile_pool(name="wq_pool", bufs=3))
        wkv_pool = ctx.enter_context(tc.tile_pool(name="wkv_pool", bufs=4))
        work = ctx.enter_context(tc.tile_pool(name="work", bufs=3))
        junk = ctx.enter_context(tc.tile_pool(name="junk", bufs=1))

        q_columns = slice(0, Q_HEADS * HEAD)
        k_columns = slice(Q_HEADS * HEAD, (Q_HEADS + KV_HEADS) * HEAD)
        v_columns = slice((Q_HEADS + KV_HEADS) * HEAD, COLUMNS)
        planes = keep.tile([P, SLOTS, COLUMNS], U8, align_bytes=64)
        nc.vector.memset(planes[:].rearrange("p j n -> p (j n)").bitcast(I32), 0)
        stage = keep.tile([P, 4, COLUMNS], U8, align_bytes=64)

        gain_rows = keep.tile([P, 2 * HEAD], BF16)
        nc.vector.memset(gain_rows[:], 0.0)
        ones = keep.tile([P, P], BF16)
        nc.vector.memset(ones[:], 1.0)
        nc.gpsimd.dma_start(out=gain_rows[0:1, 0:HEAD], in_=q_scale.unsqueeze(0))
        nc.gpsimd.dma_start(out=gain_rows[0:1, HEAD : 2 * HEAD], in_=k_scale.unsqueeze(0))

        identity = keep.tile([P, P], F32)
        make_identity(nc, identity[:])
        position_int = keep.tile([P, 1], I32)
        nc.gpsimd.iota(position_int[:], pattern=[[0, 1]], base=0, channel_multiplier=1)

        q_psum = ctx.enter_context(tc.psum_pool(name="q_psum", bufs=1, reuse_waits="tile"))
        q_acc = [
            [q_psum.tile([P, BANK], F32, name="q_acc_%d_%d" % (b, c)) for c in range(2)] for b in range(BATCH)
        ]

        x_codes = keep.tile([P, BATCH, GROUPS, P], I32, align_bytes=64)
        x_planes = keep.tile([P, BATCH, GROUPS, P], U8, align_bytes=64)

        with tc.psum_pool(name="transposed", bufs=X_BANKS, reuse_waits="tile") as transposed:

            def load_x(chunk, b):
                first_group = chunk * X_GROUPS
                x_rows = x_pool.tile([P, X_GROUPS * K_PASS], BF16, name="x_rows")
                nc.sync.dma_start(
                    out=x_rows[:],
                    in_=hidden_states[b, :, first_group * K_PASS : (first_group + X_GROUPS) * K_PASS],
                )
                parted = split_pool.tile([P, X_GROUPS, 2, P], F32, name="parted")
                nc.vector.tensor_copy(
                    out=parted[:], in_=x_rows[:].bitcast(F32).rearrange("p (g w u) -> p g u w", w=P, u=2)
                )
                return parted

            def quantise_x(parted, chunk, b):
                groups = slice(chunk * X_GROUPS, (chunk + 1) * X_GROUPS)
                grouped = grouped_pool.tile([P, X_GROUPS, P, 4], BF16, name="grouped", align_bytes=64)
                for i in range(X_BANKS):
                    bank = transposed.tile([P, BANK_GROUPS, 2, P], F32, name="bank")
                    for j in range(BANK_GROUPS):
                        for u in range(2):
                            nc.tensor.transpose(
                                bank[:, j, u, :], parted[:, i * BANK_GROUPS + j, u, :], identity[:]
                            )
                    target = (
                        grouped[:, i * BANK_GROUPS : (i + 1) * BANK_GROUPS, :, :]
                        .rearrange("p g m t -> p g (m t)")
                        .bitcast(F32)
                        .rearrange("p g (m u) -> p g m u", u=2)
                    )
                    source = bank[:].rearrange("p g u m -> p g m u")
                    if i == X_BANKS - 1:
                        nc.vector.tensor_copy(out=target, in_=source)
                    else:
                        nc.scalar.copy(out=target, in_=source)
                nc.vector.quantize_mx(
                    out=x_codes[:, b, groups, :].rearrange("p g m -> p (g m)").bitcast(FP8X4),
                    scales=x_planes[:, b, groups, :].rearrange("p g m -> p (g m)"),
                    in_=grouped[:].rearrange("p g m t -> p (g m t)"),
                )

            def load_wq(slot):
                first_group = slot * WQ_GROUPS
                words = wq_pool.tile([P, WQ_GROUPS, Q_HEADS * HEAD], I32, name="wq_tile", align_bytes=64)
                nc.sync.dma_start(
                    out=words[:],
                    in_=wq_words[first_group : first_group + WQ_GROUPS]
                    .rearrange("g p n t -> p g (n t)")
                    .bitcast(I32),
                )
                return words

            def multiply_q(words, slot):
                for j in range(WQ_GROUPS):
                    g = slot * WQ_GROUPS + j
                    for b in range(BATCH):
                        for c in range(2):
                            columns = slice(c * BANK, (c + 1) * BANK)
                            nc.tensor.matmul_mx(
                                out=q_acc[b][c][:],
                                lhsT=x_codes[:, b, g, :].bitcast(FP8X4),
                                lhsT_scale=x_planes[:, b, g, :],
                                rhs=words[:, j, columns].bitcast(FP8X4),
                                rhs_scale=plane_of(planes, g, columns),
                                start=(g == 0),
                                stop=(g == GROUPS - 1),
                            )

            x_loads = [(chunk, b) for chunk in range(GROUPS // X_GROUPS) for b in range(BATCH)]
            first = load_x(*x_loads[0])
            stage_scales(nc, stage, wq_scales, q_columns)
            second = load_x(*x_loads[1])
            quantise_x(first, *x_loads[0])
            stage_scales(nc, stage, wk_scales, k_columns)
            third = load_x(*x_loads[2])
            quantise_x(second, *x_loads[1])
            stage_scales(nc, stage, wv_scales, v_columns)
            quantise_x(third, *x_loads[2])
            for slot in range(SLOTS):
                words = load_wq(slot)
                if slot == 0:
                    place_scales(nc, planes, stage, 0, (0, 2, 1, 3))
                multiply_q(words, slot)
                if slot + 3 < len(x_loads):
                    quantise_x(load_x(*x_loads[slot + 3]), *x_loads[slot + 3])
                if slot + 1 < SLOTS:
                    place_scales(nc, planes, stage, slot + 1, (0, 2, 1, 3))
                if slot == 1:
                    gain_bank = transposed.tile([P, BANK], F32, name="bank")
                    nc.tensor.matmul(
                        out=gain_bank[:, 0 : 2 * HEAD], lhsT=ones[:], rhs=gain_rows[:], start=True, stop=True
                    )
                    gains = keep.tile([P, 2, 2, HALF], F32)
                    nc.vector.tensor_copy(
                        out=gains[:].rearrange("p w h d -> p (w h d)"), in_=gain_bank[:, 0 : 2 * HEAD]
                    )

        with tc.psum_pool(name="kv_psum", bufs=1, reuse_waits="tile") as kv_psum:
            k_acc = [kv_psum.tile([P, BANK], F32, name="k_acc_%d" % b) for b in range(BATCH)]
            v_acc = [kv_psum.tile([P, BANK], F32, name="v_acc_%d" % b) for b in range(BATCH)]

            inv_freq = keep.tile([P, HALF], F32)
            nc.vector.memset(inv_freq[:, 0:1], 1.0)
            width = 1
            while width < HALF:
                nc.vector.tensor_scalar_mul(
                    out=inv_freq[:, width : 2 * width],
                    in0=inv_freq[:, 0:width],
                    scalar1=WAVELENGTH ** (-width / HALF),
                )
                width *= 2
            position = keep.tile([P, 1], F32)
            nc.vector.tensor_copy(out=position[:], in_=position_int[:])
            angle = keep.tile([P, HALF], F32)
            nc.vector.tensor_scalar_mul(out=angle[:], in0=inv_freq[:], scalar1=position[:, 0:1])
            turns = keep.tile([P, HALF], F32)
            nc.vector.tensor_scalar(
                out=turns[:],
                in0=angle[:],
                scalar1=1.0 / (2.0 * math.pi),
                scalar2=ROUND_TO_WHOLE,
                op0=ALU.mult,
                op1=ALU.add,
            )
            nc.vector.tensor_scalar_add(out=turns[:], in0=turns[:], scalar1=-ROUND_TO_WHOLE)
            for piece in (TWO_PI_HIGH, TWO_PI_MID, TWO_PI_LOW):
                nc.vector.scalar_tensor_tensor(
                    out=angle[:], in0=turns[:], scalar=-piece, in1=angle[:], op0=ALU.mult, op1=ALU.add
                )
            angle_abs = keep.tile([P, HALF], F32)
            nc.vector.scalar_tensor_tensor(
                out=angle_abs[:], in0=angle[:], scalar=-1.0, in1=angle[:], op0=ALU.mult, op1=ALU.max
            )
            sin = keep.tile([P, HALF], F32)
            nc.scalar.activation(out=sin[:], in_=angle[:], func=ACT.Sin)
            cos = keep.tile([P, HALF], F32)
            nc.scalar.activation(out=cos[:], in_=angle_abs[:], func=ACT.Sin, bias=math.pi / 2.0, scale=-1.0)
            sqrt_warm = keep.tile([P, 1], F32)
            nc.scalar.activation(out=sqrt_warm[:], in_=position[:], func=ACT.Sqrt)
            same = keep.tile([P, 2, 2, HALF], F32)
            other = keep.tile([P, 2, 2, HALF], F32)
            for w in range(2):
                nc.vector.tensor_tensor(
                    out=same[:, w, :, :],
                    in0=gains[:, w, :, :],
                    in1=cos[:].unsqueeze(1).to_broadcast([P, 2, HALF]),
                    op=ALU.mult,
                )
                nc.vector.scalar_tensor_tensor(
                    out=other[:, w, 0, :], in0=gains[:, w, 1, :], scalar=-1.0, in1=sin[:], op0=ALU.mult, op1=ALU.mult
                )
                nc.vector.tensor_tensor(out=other[:, w, 1, :], in0=gains[:, w, 0, :], in1=sin[:], op=ALU.mult)

            def root_mean_squares(acc, heads):
                squares = junk.tile([P, BANK], F32, name="squares")
                sums = work.tile([P, 4], F32, name="sums")
                for h in range(heads):
                    columns = slice(h * HEAD, (h + 1) * HEAD)
                    nc.scalar.activation(
                        out=squares[:, columns], in_=acc[:, columns], func=ACT.Square, accum_out=sums[:, h : h + 1]
                    )
                rms = work.tile([P, 4], F32, name="rms")
                nc.scalar.activation(
                    out=rms[:, 0:heads], in_=sums[:, 0:heads], func=ACT.Sqrt, bias=EPS, scale=1.0 / HEAD
                )
                return rms

            def inverted(rms, heads):
                inverse = work.tile([P, 4], F32, name="inverse")
                nc.vector.reciprocal(out=inverse[:, 0:heads], in_=rms[:, 0:heads])
                return inverse

            def rotated(acc, heads, w):
                sums = acc[:, 0 : heads * HEAD].rearrange("p (h d) -> p h d", d=HEAD)
                halves = acc[:, 0 : heads * HEAD].rearrange("p (h s d) -> p h s d", s=2, d=HALF)
                turned = work.tile([P, 4, 2, HALF], F32, name="turned")
                crossed = work.tile([P, 4, 2, HALF], F32, name="crossed")
                nc.vector.tensor_tensor(
                    out=turned[:, 0:heads, :, :].rearrange("p h s d -> p h (s d)"),
                    in0=sums,
                    in1=same[:, w, :, :].rearrange("p s d -> p (s d)").unsqueeze(1).to_broadcast([P, heads, HEAD]),
                    op=ALU.mult,
                )
                for s in range(2):
                    nc.vector.tensor_tensor(
                        out=crossed[:, 0:heads, s, :],
                        in0=halves[:, :, 1 - s, :],
                        in1=other[:, w, s, :].unsqueeze(1).to_broadcast([P, heads, HALF]),
                        op=ALU.mult,
                    )
                nc.vector.tensor_tensor(
                    out=turned[:, 0:heads, :, :], in0=turned[:, 0:heads, :, :], in1=crossed[:, 0:heads, :, :], op=ALU.add
                )
                return turned

            def scale_heads(result, turned, inverse, heads):
                for h in range(heads):
                    nc.scalar.activation(
                        out=result[:, h, :],
                        in_=turned[:, h, :, :].rearrange("p s d -> p (s d)"),
                        func=ACT.Copy,
                        scale=inverse[:, h : h + 1],
                    )

            q_results = keep.tile([P, BATCH, Q_HEADS, HEAD], F32)
            k_results = keep.tile([P, BATCH, KV_HEADS, HEAD], F32)
            v_results = keep.tile([P, BATCH, KV_HEADS, HEAD], F32)
            waiting = None
            for b in range(BATCH):
                for c in range(2):
                    rms = root_mean_squares(q_acc[b][c], 4)
                    turned = rotated(q_acc[b][c], 4, 0)
                    if waiting is not None:
                        scale_heads(*waiting)
                    waiting = (q_results[:, b, 4 * c : 4 * c + 4, :], turned, inverted(rms, 4), 4)
            scale_heads(*waiting)

            kv_width = KV_HEADS * HEAD
            for w_words, columns, acc, loads in (
                (wk_words, k_columns, k_acc, WK_LOADS),
                (wv_words, v_columns, v_acc, WV_LOADS),
            ):
                for n, count in enumerate(loads):
                    first_group = sum(loads[:n])
                    if count == WK_LOADS[0]:
                        words = wkv_pool.tile([P, count, kv_width], I32, name="wkv_tile", align_bytes=64)
                    else:
                        words = keep.tile([P, count, kv_width], I32, name="wv_tile_%d" % n, align_bytes=64)
                    nc.sync.dma_start(
                        out=words[:],
                        in_=w_words[first_group : first_group + count]
                        .rearrange("g p n t -> p g (n t)")
                        .bitcast(I32),
                    )
                    for b in range(BATCH):
                        for j in range(count):
                            g = first_group + j
                            nc.tensor.matmul_mx(
                                out=acc[b][:, 0:kv_width],
                                lhsT=x_codes[:, b, g, :].bitcast(FP8X4),
                                lhsT_scale=x_planes[:, b, g, :],
                                rhs=words[:, j, :].bitcast(FP8X4),
                                rhs_scale=plane_of(planes, g, columns),
                                start=(g == 0),
                                stop=(g == GROUPS - 1),
                            )
                if acc is k_acc:
                    steps = [
                        (root_mean_squares(k_acc[b], KV_HEADS), rotated(k_acc[b], KV_HEADS, 1)) for b in range(BATCH)
                    ]
                    for b, (rms, turned) in enumerate(steps):
                        scale_heads(k_results[:, b, :, :], turned, inverted(rms, KV_HEADS), KV_HEADS)
            for b in range(BATCH):
                nc.sync.dma_start(out=out_0[b], in_=q_results[:, b, :, :])
            for b in range(BATCH):
                nc.sync.dma_start(out=out_1[b], in_=k_results[:, b, :, :])
            for b in range(BATCH):
                inverse = inverted(root_mean_squares(v_acc[b], KV_HEADS), KV_HEADS)
                nc.vector.tensor_tensor(
                    out=v_results[:, b, :, :],
                    in0=v_acc[b][:, 0 : KV_HEADS * HEAD].rearrange("p (h d) -> p h d", d=HEAD),
                    in1=inverse[:, 0:KV_HEADS].unsqueeze(2).to_broadcast([P, KV_HEADS, HEAD]),
                    op=ALU.mult,
                )
                nc.sync.dma_start(out=out_2[b], in_=v_results[:, b, :, :])
